import numpy as np
import ml_dtypes


def mxq(x, axis, fmt="e4m3"):
    dtype, down = {"e4m3": (ml_dtypes.float8_e4m3fn, 7), "e5m2": (ml_dtypes.float8_e5m2, 14)}[fmt]
    v = np.moveaxis(np.asarray(x, np.float32).astype(ml_dtypes.bfloat16).astype(np.float64), axis, -1)
    blocks = v.reshape(v.shape[:-1] + (-1, 32))
    amax = np.abs(blocks).max(-1, keepdims=True)
    byte = np.maximum(np.where(amax > 0, np.frexp(amax)[1] - 1 + 127, 0) - down, 1)
    scale = np.exp2(byte - 127.0)
    codes = (blocks / scale).astype(np.float32).astype(dtype).astype(np.float64)
    return np.moveaxis((codes * scale).reshape(v.shape), -1, axis)


WIDE = False


def mx_kscale(k):
    if not WIDE:
        return np.ones(k)
    levels = np.array([10, -10, 5, -5, 0])
    a = np.random.permutation(np.resize(levels, k // 512 * 4)).reshape(k // 512, 4)
    idx = np.arange(k)
    return np.exp2(a[idx // 512, idx % 128 // 32])


BF16 = ml_dtypes.bfloat16


def bf(x):
    return np.asarray(x, np.float32).astype(BF16)


def f64(x):
    return np.asarray(x).astype(np.float64)


B, T, C, HS, DW, DA, DV, DG = 4, 128, 512, 64, 128, 128, 128, 256


def sigmoid(z):
    return 1.0 / (1.0 + np.exp(-z))


def setup_inputs():
    s = mx_kscale(C)
    return {
        "x": bf(np.random.standard_normal((B, T, C)) * s),
        "v_first": bf(np.random.standard_normal((B, T, C))),
        "x_v": bf(np.random.uniform(0.0, 1.0, C)),
        "Wv": bf(np.random.standard_normal((C, C)) / np.sqrt(C) / s[None, :]),
        "v0": bf(np.random.standard_normal(C)),
        "xv_v1": bf(0.8 * np.random.standard_normal((B, T, DV))),
        "v2": bf(np.random.standard_normal((DV, C)) / np.sqrt(DV)),
    }


def reference(x, v_first, x_v, Wv, v0, xv_v1, v2):
    x = f64(x)
    xprev = np.concatenate([np.zeros_like(x[:, :1]), x[:, :-1]], axis=1)
    xx = xprev - x
    xv = x + xx * f64(x_v)
    v = mxq(xv, 2, "e4m3") @ mxq(f64(Wv), 1, "e4m3").T
    v = v + (f64(v_first) - v) * sigmoid(f64(v0) + f64(xv_v1) @ f64(v2))
    return v

@@ -1,0 +1,193 @@
+from contextlib import ExitStack
+
+import concourse.mybir as mybir
+from concourse.masks import make_identity
+
+BF16 = mybir.dt.bfloat16
+F32 = mybir.dt.float32
+U32 = mybir.dt.uint32
+U8 = mybir.dt.uint8
+FP8X4 = mybir.dt.float8_e4m3fn_x4
+ALU = mybir.AluOpType
+ACT = mybir.ActivationFunctionType
+
+P = 128
+B, T, C, DV = 4, 128, 512, 128
+PACK = 4
+HALVES = 2
+ROWS = 256
+WORDS = C // 2
+
+FLOPS = 2 * B * T * C * C + 2 * B * T * DV * C
+
+
+def tile_full_tmix_params_pb_s_kernel(tc, x, v_first, x_v, Wv, v0, xv_v1, v2, out):
+    nc = tc.nc
+    with ExitStack() as ctx:
+        keep = ctx.enter_context(tc.tile_pool(name="keep", bufs=1))
+        banks = ctx.enter_context(tc.psum_pool(name="banks", bufs=8))
+
+        v0_col = keep.tile([P, C // P], BF16)
+        with nc.allow_non_contiguous_dma(reason="512 single elements, once"):
+            nc.scalar.dma_start(out=v0_col[:], in_=v0.rearrange("(m p) -> p m", p=P))
+        mix_bf = keep.tile([P, PACK], BF16)
+        nc.scalar.dma_start(
+            out=mix_bf[:].rearrange("p (u e) -> p u e", e=2),
+            in_=x_v.rearrange("(u p e) -> p u e", u=2, e=2),
+        )
+        a_sb = keep.tile([P, B * DV], BF16)
+        nc.sync.dma_start(out=a_sb[:].rearrange("t (b k) -> t b k", b=B), in_=xv_v1.rearrange("b t k -> t b k"))
+        v2_sb = keep.tile([P, C], BF16)
+        nc.sync.dma_start(out=v2_sb[:], in_=v2)
+        x_sb = keep.tile([P, B * C], BF16)
+        for h in range(HALVES):
+            nc.sync.dma_start(
+                out=x_sb[:, 2 * h * C : (2 * h + 2) * C].rearrange("t (b c) -> t b c", b=2),
+                in_=x[2 * h : 2 * h + 2].rearrange("b t c -> t b c"),
+            )
+        w_sb = keep.tile([P, 4 * C], BF16)
+        for h in range(HALVES):
+            nc.sync.dma_start(
+                out=w_sb[:, 2 * h * C : (2 * h + 2) * C].rearrange("o (m k) -> o m k", m=2),
+                in_=Wv[h * ROWS : (h + 1) * ROWS, :].rearrange("(m o) k -> o m k", o=P),
+            )
+        vf_sb = keep.tile([P, B, C], BF16)
+        nc.sync.dma_start(out=vf_sb[:], in_=v_first.rearrange("b t c -> t b c"))
+
+        warm = keep.tile([P, 1], F32)
+        nc.vector.memset(warm[:], 0.0)
+        nc.scalar.activation(out=warm[:], in_=warm[:], func=ACT.Sigmoid)
+
+        ident_bf = keep.tile([P, P], BF16)
+        make_identity(nc, ident_bf[:])
+        ident_f32 = keep.tile([P, P], F32)
+        make_identity(nc, ident_f32[:])
+
+        mix = keep.tile([P, PACK], F32)
+        nc.vector.tensor_copy(out=mix[:], in_=mix_bf[:])
+        stay = keep.tile([P, PACK], F32)
+        nc.vector.tensor_scalar(out=stay[:], in0=mix[:], scalar1=-1.0, scalar2=1.0, op0=ALU.mult, op1=ALU.add)
+
+        aT_ps = banks.tile([P, B * T], BF16, tag="bank")
+        for b in range(B):
+            nc.tensor.transpose(aT_ps[:, b * T : (b + 1) * T], a_sb[:, b * DV : (b + 1) * DV], ident_bf[:])
+        aT = keep.tile([P, B * T], BF16)
+        nc.vector.tensor_copy(out=aT[:], in_=aT_ps[:])
+
+        v0_rep = keep.tile([P, C // P, P], F32)
+        nc.vector.tensor_copy(out=v0_rep[:], in_=v0_col[:].unsqueeze(2).to_broadcast([P, C // P, P]))
+        v0_ps = banks.tile([P, C], F32, tag="bank")
+        for m in range(C // P):
+            nc.tensor.transpose(v0_ps[:, m * P : (m + 1) * P], v0_rep[:, m, :], ident_f32[:])
+        v0_all = keep.tile([P, C], F32)
+        nc.vector.tensor_copy(out=v0_all[:], in_=v0_ps[:])
+
+        pre = keep.tile([P, B, C], F32)
+        gate = keep.tile([P, B, C], F32)
+        from_first = keep.tile([P, B, C], F32)
+        for b in range(B):
+            z = banks.tile([P, C], F32, tag="bank")
+            nc.tensor.matmul(out=z[:], lhsT=aT[:, b * T : (b + 1) * T], rhs=v2_sb[:], start=True, stop=True)
+            nc.vector.tensor_tensor(out=pre[:, b, :], in0=z[:], in1=v0_all[:], op=ALU.add)
+            nc.scalar.activation(out=gate[:, b, :], in_=pre[:, b, :], func=ACT.Sigmoid)
+            nc.gpsimd.tensor_tensor(out=from_first[:, b, :], in0=vf_sb[:, b, :], in1=gate[:, b, :], op=ALU.mult)
+
+        x_words = x_sb[:].bitcast(F32)
+        kept = keep.tile([P, HALVES, PACK, ROWS], F32)
+        xv_slot = keep.tile([P, HALVES, PACK, ROWS], BF16)
+        xv_grp = keep.tile([P, HALVES, ROWS, PACK], BF16, align_bytes=64)
+        x_codes = keep.tile([P, B * T], U32, align_bytes=64)
+        x_scales = keep.tile([P, B * T], U8, align_bytes=64)
+
+        def transpose_words(words, h):
+            bank = banks.tile([P, 2 * ROWS], F32, tag="bank", name="bank")
+            view = bank[:].rearrange("p (u l r) -> p u l r", u=2, l=2)
+            for l in range(2):
+                for u in range(2):
+                    first = (2 * h + l) * WORDS + u * P
+                    nc.tensor.transpose(view[:, u, l, :], words[:, first : first + P], ident_f32[:])
+            return bank
+
+        def lerp(h):
+            bank = transpose_words(x_words, h)
+            xT = bank[:].bitcast(BF16).rearrange("p (u l t e) -> p u l t e", u=2, l=2, e=2)
+            for j in range(PACK):
+                u, e = divmod(j, 2)
+                nc.scalar.activation(
+                    out=kept[:, h, j, :].rearrange("p (l t) -> p l t", l=2),
+                    in_=xT[:, u, :, :, e],
+                    func=ACT.Copy,
+                    scale=stay[:, j : j + 1],
+                )
+            for j in range(PACK):
+                u, e = divmod(j, 2)
+                nc.vector.scalar_tensor_tensor(
+                    out=xv_slot[:, h, j, :].rearrange("p (l t) -> p l t", l=2)[:, :, 1:T],
+                    in0=xT[:, u, :, 0 : T - 1, e],
+                    scalar=mix[:, j : j + 1],
+                    in1=kept[:, h, j, :].rearrange("p (l t) -> p l t", l=2)[:, :, 1:T],
+                    op0=ALU.mult,
+                    op1=ALU.add,
+                )
+            nc.vector.tensor_copy(
+                out=xv_slot[:, h].rearrange("p j (l t) -> p j l t", l=2)[:, :, :, 0],
+                in_=kept[:, h].rearrange("p j (l t) -> p j l t", l=2)[:, :, :, 0],
+            )
+
+        def regroup(h):
+            nc.vector.tensor_copy(
+                out=xv_grp[:, h].rearrange("p (c i) j -> p c j i", i=4),
+                in_=xv_slot[:, h].rearrange("p j (c i) -> p c j i", i=4),
+            )
+
+        def quantise_x(h):
+            cols = slice(h * ROWS, (h + 1) * ROWS)
+            nc.vector.quantize_mx(
+                out=x_codes[:, cols].bitcast(FP8X4),
+                scales=x_scales[:, cols],
+                in_=xv_grp[:, h].rearrange("p r j -> p (r j)"),
+            )
+
+        w_words = w_sb[:].bitcast(F32)
+        w_grp = keep.tile([P, C * PACK], BF16, align_bytes=64)
+        w_grp_words = w_grp[:].bitcast(F32).rearrange("p (o u) -> p o u", u=2)
+        w_codes = keep.tile([P, C], U32, align_bytes=64)
+        w_scales = keep.tile([P, C], U8, align_bytes=64)
+
+        def weights(h):
+            bank = transpose_words(w_words, h)
+            nc.scalar.copy(
+                out=w_grp_words[:, h * ROWS : (h + 1) * ROWS, :],
+                in_=bank[:].rearrange("p (u o) -> p o u", u=2),
+            )
+
+        lerp(0)
+        regroup(0)
+        lerp(1)
+        quantise_x(0)
+        regroup(1)
+        weights(0)
+        weights(1)
+        nc.vector.quantize_mx(out=w_codes[:].bitcast(FP8X4), scales=w_scales[:], in_=w_grp[:])
+        quantise_x(1)
+
+        minus_p = keep.tile([P, B, C], F32)
+        res = keep.tile([P, B, C], F32)
+        for b in range(B):
+            toks = slice(b * T, (b + 1) * T)
+            p_ps = banks.tile([P, C], F32, tag="bank")
+            nc.tensor.matmul_mx(
+                out=p_ps[:],
+                lhsT=x_codes[:, toks].bitcast(FP8X4),
+                lhsT_scale=x_scales[:, toks],
+                rhs=w_codes[:].bitcast(FP8X4),
+                rhs_scale=w_scales[:],
+                start=True,
+                stop=True,
+            )
+            nc.vector.scalar_tensor_tensor(
+                out=minus_p[:, b, :], in0=gate[:, b, :], scalar=1.0, in1=p_ps[:], op0=ALU.subtract, op1=ALU.mult
+            )
+            engine = nc.gpsimd if b < B // 2 else nc.vector
+            engine.tensor_tensor(out=res[:, b, :], in0=from_first[:, b, :], in1=minus_p[:, b, :], op=ALU.subtract)
+            nc.sync.dma_start(out=out[b], in_=res[:, b, :])

@@ -26,25 +26,26 @@ def tile_full_tmix_params_pb_s_kernel(tc, x, v_first, x_v, Wv, v0, xv_v1, v2, ou
     with ExitStack() as ctx:
         keep = ctx.enter_context(tc.tile_pool(name="keep", bufs=1))
         banks = ctx.enter_context(tc.psum_pool(name="banks", bufs=8))
+        ctx.enter_context(tc.manual_schedule())
 
-        v0_col = keep.tile([P, C // P], BF16)
-        with nc.allow_non_contiguous_dma(reason="512 single elements, once"):
-            nc.scalar.dma_start(out=v0_col[:], in_=v0.rearrange("(m p) -> p m", p=P))
         mix_bf = keep.tile([P, PACK], BF16)
         nc.scalar.dma_start(
             out=mix_bf[:].rearrange("p (u e) -> p u e", e=2),
             in_=x_v.rearrange("(u p e) -> p u e", u=2, e=2),
         )
+        v0_col = keep.tile([P, C // P], BF16)
+        with nc.allow_non_contiguous_dma(reason="512 single elements, once"):
+            nc.scalar.dma_start(out=v0_col[:], in_=v0.rearrange("(m p) -> p m", p=P))
         a_sb = keep.tile([P, B * DV], BF16)
         nc.sync.dma_start(out=a_sb[:].rearrange("t (b k) -> t b k", b=B), in_=xv_v1.rearrange("b t k -> t b k"))
-        v2_sb = keep.tile([P, C], BF16)
-        nc.sync.dma_start(out=v2_sb[:], in_=v2)
         x_sb = keep.tile([P, B * C], BF16)
         for h in range(HALVES):
             nc.sync.dma_start(
                 out=x_sb[:, 2 * h * C : (2 * h + 2) * C].rearrange("t (b c) -> t b c", b=2),
                 in_=x[2 * h : 2 * h + 2].rearrange("b t c -> t b c"),
             )
+        v2_sb = keep.tile([P, C], BF16)
+        nc.sync.dma_start(out=v2_sb[:], in_=v2)
         w_sb = keep.tile([P, 4 * C], BF16)
         for h in range(HALVES):
             nc.sync.dma_start(
@@ -67,68 +68,56 @@ def tile_full_tmix_params_pb_s_kernel(tc, x, v_first, x_v, Wv, v0, xv_v1, v2, ou
         nc.vector.tensor_copy(out=mix[:], in_=mix_bf[:])
         stay = keep.tile([P, PACK], F32)
         nc.vector.tensor_scalar(out=stay[:], in0=mix[:], scalar1=-1.0, scalar2=1.0, op0=ALU.mult, op1=ALU.add)
-
-        aT_ps = banks.tile([P, B * T], BF16, tag="bank")
-        for b in range(B):
-            nc.tensor.transpose(aT_ps[:, b * T : (b + 1) * T], a_sb[:, b * DV : (b + 1) * DV], ident_bf[:])
-        aT = keep.tile([P, B * T], BF16)
-        nc.vector.tensor_copy(out=aT[:], in_=aT_ps[:])
-
         v0_rep = keep.tile([P, C // P, P], F32)
         nc.vector.tensor_copy(out=v0_rep[:], in_=v0_col[:].unsqueeze(2).to_broadcast([P, C // P, P]))
-        v0_ps = banks.tile([P, C], F32, tag="bank")
-        for m in range(C // P):
-            nc.tensor.transpose(v0_ps[:, m * P : (m + 1) * P], v0_rep[:, m, :], ident_f32[:])
-        v0_all = keep.tile([P, C], F32)
-        nc.vector.tensor_copy(out=v0_all[:], in_=v0_ps[:])
 
-        pre = keep.tile([P, B, C], F32)
+        aT = keep.tile([P, B * T], BF16)
         gate = keep.tile([P, B, C], F32)
         from_first = keep.tile([P, B, C], F32)
-        for b in range(B):
-            z = banks.tile([P, C], F32, tag="bank")
-            nc.tensor.matmul(out=z[:], lhsT=aT[:, b * T : (b + 1) * T], rhs=v2_sb[:], start=True, stop=True)
-            nc.vector.tensor_tensor(out=pre[:, b, :], in0=z[:], in1=v0_all[:], op=ALU.add)
-            nc.scalar.activation(out=gate[:, b, :], in_=pre[:, b, :], func=ACT.Sigmoid)
-            nc.gpsimd.tensor_tensor(out=from_first[:, b, :], in0=vf_sb[:, b, :], in1=gate[:, b, :], op=ALU.mult)
-
         x_words = x_sb[:].bitcast(F32)
         kept = keep.tile([P, HALVES, PACK, ROWS], F32)
         xv_slot = keep.tile([P, HALVES, PACK, ROWS], BF16)
         xv_grp = keep.tile([P, HALVES, ROWS, PACK], BF16, align_bytes=64)
         x_codes = keep.tile([P, B * T], U32, align_bytes=64)
         x_scales = keep.tile([P, B * T], U8, align_bytes=64)
+        w_words = w_sb[:].bitcast(F32)
+        w_grp = keep.tile([P, C * PACK], BF16, align_bytes=64)
+        w_grp_words = w_grp[:].bitcast(F32).rearrange("p (o u) -> p o u", u=2)
+        w_codes = keep.tile([P, C], U32, align_bytes=64)
+        w_scales = keep.tile([P, C], U8, align_bytes=64)
+        minus_p = keep.tile([P, B, C], F32)
+        res = keep.tile([P, B, C], F32)
 
-        def transpose_words(words, h):
-            bank = banks.tile([P, 2 * ROWS], F32, tag="bank", name="bank")
-            view = bank[:].rearrange("p (u l r) -> p u l r", u=2, l=2)
+        def by_sequence(plane):
+            return plane.rearrange("p (l t) -> p l t", l=2)
+
+        def transpose_x(h, u):
+            bank = banks.tile([P, ROWS], F32, tag="bank", name="x_bank")
             for l in range(2):
-                for u in range(2):
-                    first = (2 * h + l) * WORDS + u * P
-                    nc.tensor.transpose(view[:, u, l, :], words[:, first : first + P], ident_f32[:])
-            return bank
+                first = (2 * h + l) * WORDS + u * P
+                nc.tensor.transpose(bank[:, l * T : (l + 1) * T], x_words[:, first : first + P], ident_f32[:])
+            return bank[:].bitcast(BF16).rearrange("p (l t e) -> p l t e", l=2, e=2)
 
-        def lerp(h):
-            bank = transpose_words(x_words, h)
-            xT = bank[:].bitcast(BF16).rearrange("p (u l t e) -> p u l t e", u=2, l=2, e=2)
-            for j in range(PACK):
-                u, e = divmod(j, 2)
+        def keep_part(h, u, xT):
+            for e in range(2):
+                j = 2 * u + e
                 nc.scalar.activation(
-                    out=kept[:, h, j, :].rearrange("p (l t) -> p l t", l=2),
-                    in_=xT[:, u, :, :, e],
-                    func=ACT.Copy,
-                    scale=stay[:, j : j + 1],
+                    out=by_sequence(kept[:, h, j, :]), in_=xT[:, :, :, e], func=ACT.Copy, scale=stay[:, j : j + 1]
                 )
-            for j in range(PACK):
-                u, e = divmod(j, 2)
+
+        def add_previous(h, u, xT):
+            for e in range(2):
+                j = 2 * u + e
                 nc.vector.scalar_tensor_tensor(
-                    out=xv_slot[:, h, j, :].rearrange("p (l t) -> p l t", l=2)[:, :, 1:T],
-                    in0=xT[:, u, :, 0 : T - 1, e],
+                    out=by_sequence(xv_slot[:, h, j, :])[:, :, 1:T],
+                    in0=xT[:, :, 0 : T - 1, e],
                     scalar=mix[:, j : j + 1],
-                    in1=kept[:, h, j, :].rearrange("p (l t) -> p l t", l=2)[:, :, 1:T],
+                    in1=by_sequence(kept[:, h, j, :])[:, :, 1:T],
                     op0=ALU.mult,
                     op1=ALU.add,
                 )
+
+        def first_tokens(h):
             nc.vector.tensor_copy(
                 out=xv_slot[:, h].rearrange("p j (l t) -> p j l t", l=2)[:, :, :, 0],
                 in_=kept[:, h].rearrange("p j (l t) -> p j l t", l=2)[:, :, :, 0],
@@ -148,31 +137,63 @@ def tile_full_tmix_params_pb_s_kernel(tc, x, v_first, x_v, Wv, v0, xv_v1, v2, ou
                 in_=xv_grp[:, h].rearrange("p r j -> p (r j)"),
             )
 
-        w_words = w_sb[:].bitcast(F32)
-        w_grp = keep.tile([P, C * PACK], BF16, align_bytes=64)
-        w_grp_words = w_grp[:].bitcast(F32).rearrange("p (o u) -> p o u", u=2)
-        w_codes = keep.tile([P, C], U32, align_bytes=64)
-        w_scales = keep.tile([P, C], U8, align_bytes=64)
-
         def weights(h):
-            bank = transpose_words(w_words, h)
+            bank = banks.tile([P, 2 * ROWS], F32, tag="bank", name="w_bank")
+            view = bank[:].rearrange("p (u l o) -> p u l o", u=2, l=2)
+            for l in range(2):
+                for u in range(2):
+                    first = (2 * h + l) * WORDS + u * P
+                    nc.tensor.transpose(view[:, u, l, :], w_words[:, first : first + P], ident_f32[:])
             nc.scalar.copy(
                 out=w_grp_words[:, h * ROWS : (h + 1) * ROWS, :],
                 in_=bank[:].rearrange("p (u o) -> p o u", u=2),
             )
 
-        lerp(0)
-        regroup(0)
-        lerp(1)
-        quantise_x(0)
-        regroup(1)
+        def gate_of(b):
+            z = banks.tile([P, C], F32, tag="bank", name="z")
+            for m in range(C // P):
+                nc.tensor.matmul(
+                    out=z[:, m * P : (m + 1) * P],
+                    lhsT=v0_rep[:, m, :],
+                    rhs=ident_f32[:],
+                    is_transpose=True,
+                    start=(m == 0),
+                    stop=False,
+                )
+            nc.tensor.matmul(out=z[:], lhsT=aT[:, b * T : (b + 1) * T], rhs=v2_sb[:], start=False, stop=True)
+            nc.scalar.activation(out=gate[:, b, :], in_=z[:], func=ACT.Sigmoid)
+            nc.gpsimd.tensor_tensor(out=from_first[:, b, :], in0=vf_sb[:, b, :], in1=gate[:, b, :], op=ALU.mult)
+
+        aT_ps = banks.tile([P, B * T], BF16, tag="bank")
+        for b in range(B):
+            nc.tensor.transpose(aT_ps[:, b * T : (b + 1) * T], a_sb[:, b * DV : (b + 1) * DV], ident_bf[:])
+        nc.vector.tensor_copy(out=aT[:], in_=aT_ps[:])
+
+        pieces = [(h, u) for h in range(HALVES) for u in range(2)]
+        xT = {}
+        for h, u in pieces:
+            xT[(h, u)] = transpose_x(h, u)
+        for h, u in pieces:
+            keep_part(h, u, xT[(h, u)])
+        gate_of(0)
+        gate_of(1)
         weights(0)
         weights(1)
+        gate_of(2)
+        gate_of(3)
+
+        add_previous(0, 0, xT[(0, 0)])
+        add_previous(0, 1, xT[(0, 1)])
+        first_tokens(0)
+        regroup(0)
+        add_previous(1, 0, xT[(1, 0)])
+        add_previous(1, 1, xT[(1, 1)])
+        quantise_x(0)
+        first_tokens(1)
+        regroup(1)
         nc.vector.quantize_mx(out=w_codes[:].bitcast(FP8X4), scales=w_scales[:], in_=w_grp[:])
         quantise_x(1)
 
-        minus_p = keep.tile([P, B, C], F32)
-        res = keep.tile([P, B, C], F32)
         for b in range(B):
             toks = slice(b * T, (b + 1) * T)
             p_ps = banks.tile([P, C], F32, tag="bank")

@@ -209,6 +209,5 @@ def tile_full_tmix_params_pb_s_kernel(tc, x, v_first, x_v, Wv, v0, xv_v1, v2, ou
             nc.vector.scalar_tensor_tensor(
                 out=minus_p[:, b, :], in0=gate[:, b, :], scalar=1.0, in1=p_ps[:], op0=ALU.subtract, op1=ALU.mult
             )
-            engine = nc.gpsimd if b < B // 2 else nc.vector
-            engine.tensor_tensor(out=res[:, b, :], in0=from_first[:, b, :], in1=minus_p[:, b, :], op=ALU.subtract)
+            nc.vector.tensor_tensor(out=res[:, b, :], in0=from_first[:, b, :], in1=minus_p[:, b, :], op=ALU.subtract)
             nc.sync.dma_start(out=out[b], in_=res[:, b, :])

@@ -185,11 +185,11 @@ def tile_full_tmix_params_pb_s_kernel(tc, x, v_first, x_v, Wv, v0, xv_v1, v2, ou
         add_previous(0, 0, xT[(0, 0)])
         add_previous(0, 1, xT[(0, 1)])
         first_tokens(0)
-        regroup(0)
         add_previous(1, 0, xT[(1, 0)])
+        regroup(0)
         add_previous(1, 1, xT[(1, 1)])
-        quantise_x(0)
         first_tokens(1)
+        quantise_x(0)
         regroup(1)
         nc.vector.quantize_mx(out=w_codes[:].bitcast(FP8X4), scales=w_scales[:], in_=w_grp[:])
         quantise_x(1)
@@ -209,5 +209,7 @@ def tile_full_tmix_params_pb_s_kernel(tc, x, v_first, x_v, Wv, v0, xv_v1, v2, ou
             nc.vector.scalar_tensor_tensor(
                 out=minus_p[:, b, :], in0=gate[:, b, :], scalar=1.0, in1=p_ps[:], op0=ALU.subtract, op1=ALU.mult
             )
-            nc.vector.tensor_tensor(out=res[:, b, :], in0=from_first[:, b, :], in1=minus_p[:, b, :], op=ALU.subtract)
+        for b in range(B):
+            engine = nc.gpsimd if b == 0 else nc.vector
+            engine.tensor_tensor(out=res[:, b, :], in0=from_first[:, b, :], in1=minus_p[:, b, :], op=ALU.subtract)
             nc.sync.dma_start(out=out[b], in_=res[:, b, :])

@@ -210,6 +210,6 @@ def tile_full_tmix_params_pb_s_kernel(tc, x, v_first, x_v, Wv, v0, xv_v1, v2, ou
                 out=minus_p[:, b, :], in0=gate[:, b, :], scalar=1.0, in1=p_ps[:], op0=ALU.subtract, op1=ALU.mult
             )
         for b in range(B):
-            engine = nc.gpsimd if b == 0 else nc.vector
+            engine = nc.gpsimd if b < B - 1 else nc.vector
             engine.tensor_tensor(out=res[:, b, :], in0=from_first[:, b, :], in1=minus_p[:, b, :], op=ALU.subtract)
             nc.sync.dma_start(out=out[b], in_=res[:, b, :])

@@ -210,6 +210,6 @@ def tile_full_tmix_params_pb_s_kernel(tc, x, v_first, x_v, Wv, v0, xv_v1, v2, ou
                 out=minus_p[:, b, :], in0=gate[:, b, :], scalar=1.0, in1=p_ps[:], op0=ALU.subtract, op1=ALU.mult
             )
         for b in range(B):
-            engine = nc.gpsimd if b < B - 1 else nc.vector
+            engine = nc.gpsimd if b < B // 2 else nc.vector
             engine.tensor_tensor(out=res[:, b, :], in0=from_first[:, b, :], in1=minus_p[:, b, :], op=ALU.subtract)
             nc.sync.dma_start(out=out[b], in_=res[:, b, :])

@@ -185,11 +185,11 @@ def tile_full_tmix_params_pb_s_kernel(tc, x, v_first, x_v, Wv, v0, xv_v1, v2, ou
         add_previous(0, 0, xT[(0, 0)])
         add_previous(0, 1, xT[(0, 1)])
         first_tokens(0)
-        add_previous(1, 0, xT[(1, 0)])
         regroup(0)
+        add_previous(1, 0, xT[(1, 0)])
         add_previous(1, 1, xT[(1, 1)])
-        first_tokens(1)
         quantise_x(0)
+        first_tokens(1)
         regroup(1)
         nc.vector.quantize_mx(out=w_codes[:].bitcast(FP8X4), scales=w_scales[:], in_=w_grp[:])
         quantise_x(1)
@@ -209,7 +209,7 @@ def tile_full_tmix_params_pb_s_kernel(tc, x, v_first, x_v, Wv, v0, xv_v1, v2, ou
             nc.vector.scalar_tensor_tensor(
                 out=minus_p[:, b, :], in0=gate[:, b, :], scalar=1.0, in1=p_ps[:], op0=ALU.subtract, op1=ALU.mult
             )
-        for b in range(B):
             engine = nc.gpsimd if b < B // 2 else nc.vector
             engine.tensor_tensor(out=res[:, b, :], in0=from_first[:, b, :], in1=minus_p[:, b, :], op=ALU.subtract)
-            nc.sync.dma_start(out=out[b], in_=res[:, b, :])
+            queue = nc.scalar if b < B // 2 else nc.sync
+            queue.dma_start(out=out[b], in_=res[:, b, :])

from contextlib import ExitStack

import concourse.mybir as mybir
from concourse.masks import make_identity

BF16 = mybir.dt.bfloat16
F32 = mybir.dt.float32
U32 = mybir.dt.uint32
U8 = mybir.dt.uint8
FP8X4 = mybir.dt.float8_e4m3fn_x4
ALU = mybir.AluOpType
ACT = mybir.ActivationFunctionType

P = 128
B, T, C, DV = 4, 128, 512, 128
PACK = 4
HALVES = 2
ROWS = 256
WORDS = C // 2

FLOPS = 2 * B * T * C * C + 2 * B * T * DV * C


def tile_full_tmix_params_pb_s_kernel(tc, x, v_first, x_v, Wv, v0, xv_v1, v2, out):
    nc = tc.nc
    with ExitStack() as ctx:
        keep = ctx.enter_context(tc.tile_pool(name="keep", bufs=1))
        banks = ctx.enter_context(tc.psum_pool(name="banks", bufs=8))
        ctx.enter_context(tc.manual_schedule())

        mix_bf = keep.tile([P, PACK], BF16)
        nc.scalar.dma_start(
            out=mix_bf[:].rearrange("p (u e) -> p u e", e=2),
            in_=x_v.rearrange("(u p e) -> p u e", u=2, e=2),
        )
        v0_col = keep.tile([P, C // P], BF16)
        with nc.allow_non_contiguous_dma(reason="512 single elements, once"):
            nc.scalar.dma_start(out=v0_col[:], in_=v0.rearrange("(m p) -> p m", p=P))
        a_sb = keep.tile([P, B * DV], BF16)
        nc.sync.dma_start(out=a_sb[:].rearrange("t (b k) -> t b k", b=B), in_=xv_v1.rearrange("b t k -> t b k"))
        x_sb = keep.tile([P, B * C], BF16)
        for h in range(HALVES):
            nc.sync.dma_start(
                out=x_sb[:, 2 * h * C : (2 * h + 2) * C].rearrange("t (b c) -> t b c", b=2),
                in_=x[2 * h : 2 * h + 2].rearrange("b t c -> t b c"),
            )
        v2_sb = keep.tile([P, C], BF16)
        nc.sync.dma_start(out=v2_sb[:], in_=v2)
        w_sb = keep.tile([P, 4 * C], BF16)
        for h in range(HALVES):
            nc.sync.dma_start(
                out=w_sb[:, 2 * h * C : (2 * h + 2) * C].rearrange("o (m k) -> o m k", m=2),
                in_=Wv[h * ROWS : (h + 1) * ROWS, :].rearrange("(m o) k -> o m k", o=P),
            )
        vf_sb = keep.tile([P, B, C], BF16)
        nc.sync.dma_start(out=vf_sb[:], in_=v_first.rearrange("b t c -> t b c"))

        warm = keep.tile([P, 1], F32)
        nc.vector.memset(warm[:], 0.0)
        nc.scalar.activation(out=warm[:], in_=warm[:], func=ACT.Sigmoid)

        ident_bf = keep.tile([P, P], BF16)
        make_identity(nc, ident_bf[:])
        ident_f32 = keep.tile([P, P], F32)
        make_identity(nc, ident_f32[:])

        mix = keep.tile([P, PACK], F32)
        nc.vector.tensor_copy(out=mix[:], in_=mix_bf[:])
        stay = keep.tile([P, PACK], F32)
        nc.vector.tensor_scalar(out=stay[:], in0=mix[:], scalar1=-1.0, scalar2=1.0, op0=ALU.mult, op1=ALU.add)
        v0_rep = keep.tile([P, C // P, P], F32)
        nc.vector.tensor_copy(out=v0_rep[:], in_=v0_col[:].unsqueeze(2).to_broadcast([P, C // P, P]))

        aT = keep.tile([P, B * T], BF16)
        gate = keep.tile([P, B, C], F32)
        from_first = keep.tile([P, B, C], F32)
        x_words = x_sb[:].bitcast(F32)
        kept = keep.tile([P, HALVES, PACK, ROWS], F32)
        xv_slot = keep.tile([P, HALVES, PACK, ROWS], BF16)
        xv_grp = keep.tile([P, HALVES, ROWS, PACK], BF16, align_bytes=64)
        x_codes = keep.tile([P, B * T], U32, align_bytes=64)
        x_scales = keep.tile([P, B * T], U8, align_bytes=64)
        w_words = w_sb[:].bitcast(F32)
        w_grp = keep.tile([P, C * PACK], BF16, align_bytes=64)
        w_grp_words = w_grp[:].bitcast(F32).rearrange("p (o u) -> p o u", u=2)
        w_codes = keep.tile([P, C], U32, align_bytes=64)
        w_scales = keep.tile([P, C], U8, align_bytes=64)
        minus_p = keep.tile([P, B, C], F32)
        res = keep.tile([P, B, C], F32)

        def by_sequence(plane):
            return plane.rearrange("p (l t) -> p l t", l=2)

        def transpose_x(h, u):
            bank = banks.tile([P, ROWS], F32, tag="bank", name="x_bank")
            for l in range(2):
                first = (2 * h + l) * WORDS + u * P
                nc.tensor.transpose(bank[:, l * T : (l + 1) * T], x_words[:, first : first + P], ident_f32[:])
            return bank[:].bitcast(BF16).rearrange("p (l t e) -> p l t e", l=2, e=2)

        def keep_part(h, u, xT):
            for e in range(2):
                j = 2 * u + e
                nc.scalar.activation(
                    out=by_sequence(kept[:, h, j, :]), in_=xT[:, :, :, e], func=ACT.Copy, scale=stay[:, j : j + 1]
                )

        def add_previous(h, u, xT):
            for e in range(2):
                j = 2 * u + e
                nc.vector.scalar_tensor_tensor(
                    out=by_sequence(xv_slot[:, h, j, :])[:, :, 1:T],
                    in0=xT[:, :, 0 : T - 1, e],
                    scalar=mix[:, j : j + 1],
                    in1=by_sequence(kept[:, h, j, :])[:, :, 1:T],
                    op0=ALU.mult,
                    op1=ALU.add,
                )

        def first_tokens(h):
            nc.vector.tensor_copy(
                out=xv_slot[:, h].rearrange("p j (l t) -> p j l t", l=2)[:, :, :, 0],
                in_=kept[:, h].rearrange("p j (l t) -> p j l t", l=2)[:, :, :, 0],
            )

        def regroup(h):
            nc.vector.tensor_copy(
                out=xv_grp[:, h].rearrange("p (c i) j -> p c j i", i=4),
                in_=xv_slot[:, h].rearrange("p j (c i) -> p c j i", i=4),
            )

        def quantise_x(h):
            cols = slice(h * ROWS, (h + 1) * ROWS)
            nc.vector.quantize_mx(
                out=x_codes[:, cols].bitcast(FP8X4),
                scales=x_scales[:, cols],
                in_=xv_grp[:, h].rearrange("p r j -> p (r j)"),
            )

        def weights(h):
            bank = banks.tile([P, 2 * ROWS], F32, tag="bank", name="w_bank")
            view = bank[:].rearrange("p (u l o) -> p u l o", u=2, l=2)
            for l in range(2):
                for u in range(2):
                    first = (2 * h + l) * WORDS + u * P
                    nc.tensor.transpose(view[:, u, l, :], w_words[:, first : first + P], ident_f32[:])
            nc.scalar.copy(
                out=w_grp_words[:, h * ROWS : (h + 1) * ROWS, :],
                in_=bank[:].rearrange("p (u o) -> p o u", u=2),
            )

        def gate_of(b):
            z = banks.tile([P, C], F32, tag="bank", name="z")
            for m in range(C // P):
                nc.tensor.matmul(
                    out=z[:, m * P : (m + 1) * P],
                    lhsT=v0_rep[:, m, :],
                    rhs=ident_f32[:],
                    is_transpose=True,
                    start=(m == 0),
                    stop=False,
                )
            nc.tensor.matmul(out=z[:], lhsT=aT[:, b * T : (b + 1) * T], rhs=v2_sb[:], start=False, stop=True)
            nc.scalar.activation(out=gate[:, b, :], in_=z[:], func=ACT.Sigmoid)
            nc.gpsimd.tensor_tensor(out=from_first[:, b, :], in0=vf_sb[:, b, :], in1=gate[:, b, :], op=ALU.mult)

        aT_ps = banks.tile([P, B * T], BF16, tag="bank")
        for b in range(B):
            nc.tensor.transpose(aT_ps[:, b * T : (b + 1) * T], a_sb[:, b * DV : (b + 1) * DV], ident_bf[:])
        nc.vector.tensor_copy(out=aT[:], in_=aT_ps[:])

        pieces = [(h, u) for h in range(HALVES) for u in range(2)]
        xT = {}
        for h, u in pieces:
            xT[(h, u)] = transpose_x(h, u)
        for h, u in pieces:
            keep_part(h, u, xT[(h, u)])
        gate_of(0)
        gate_of(1)
        weights(0)
        weights(1)
        gate_of(2)
        gate_of(3)

        add_previous(0, 0, xT[(0, 0)])
        add_previous(0, 1, xT[(0, 1)])
        first_tokens(0)
        regroup(0)
        add_previous(1, 0, xT[(1, 0)])
        add_previous(1, 1, xT[(1, 1)])
        quantise_x(0)
        first_tokens(1)
        regroup(1)
        nc.vector.quantize_mx(out=w_codes[:].bitcast(FP8X4), scales=w_scales[:], in_=w_grp[:])
        quantise_x(1)

        for b in range(B):
            toks = slice(b * T, (b + 1) * T)
            p_ps = banks.tile([P, C], F32, tag="bank")
            nc.tensor.matmul_mx(
                out=p_ps[:],
                lhsT=x_codes[:, toks].bitcast(FP8X4),
                lhsT_scale=x_scales[:, toks],
                rhs=w_codes[:].bitcast(FP8X4),
                rhs_scale=w_scales[:],
                start=True,
                stop=True,
            )
            nc.vector.scalar_tensor_tensor(
                out=minus_p[:, b, :], in0=gate[:, b, :], scalar=1.0, in1=p_ps[:], op0=ALU.subtract, op1=ALU.mult
            )
            engine = nc.gpsimd if b < B // 2 else nc.vector
            engine.tensor_tensor(out=res[:, b, :], in0=from_first[:, b, :], in1=minus_p[:, b, :], op=ALU.subtract)
            queue = nc.scalar if b < B // 2 else nc.sync
            queue.dma_start(out=out[b], in_=res[:, b, :])
